import numpy as np
import ml_dtypes


def mxq(x, axis, fmt="e4m3"):
    dtype, down = {"e4m3": (ml_dtypes.float8_e4m3fn, 7), "e5m2": (ml_dtypes.float8_e5m2, 14)}[fmt]
    v = np.moveaxis(np.asarray(x, np.float32).astype(ml_dtypes.bfloat16).astype(np.float64), axis, -1)
    blocks = v.reshape(v.shape[:-1] + (-1, 32))
    amax = np.abs(blocks).max(-1, keepdims=True)
    byte = np.maximum(np.where(amax > 0, np.frexp(amax)[1] - 1 + 127, 0) - down, 1)
    scale = np.exp2(byte - 127.0)
    codes = (blocks / scale).astype(np.float32).astype(dtype).astype(np.float64)
    return np.moveaxis((codes * scale).reshape(v.shape), -1, axis)


WIDE = False


def mx_kscale(k):
    if not WIDE:
        return np.ones(k)
    levels = np.array([10, -10, 5, -5, 0])
    a = np.random.permutation(np.resize(levels, k // 512 * 4)).reshape(k // 512, 4)
    idx = np.arange(k)
    return np.exp2(a[idx // 512, idx % 128 // 32])


BF16 = ml_dtypes.bfloat16


def bf(x):
    return np.asarray(x, np.float32).astype(BF16)


def f64(x):
    return np.asarray(x).astype(np.float64)


B, S, D, NH, LAT, F = 4, 128, 2048, 16, 512, 8192
EPS = 1e-5


def layer_norm(c, g, b):
    m = c.mean(-1, keepdims=True)
    v = ((c - m) ** 2).mean(-1, keepdims=True)
    return (c - m) * (1.0 / np.sqrt(v + EPS)) * g + b


def down_weight():
    return (np.random.standard_normal((D, LAT)) + 0.3 * np.random.standard_normal((D, 1))) / np.sqrt(D)


def setup_inputs():
    s = mx_kscale(D)
    tq, tkv = mx_kscale(LAT), mx_kscale(LAT)
    return {
        "normed": bf(np.random.standard_normal((B, S, D)) * s),
        "W_dq": bf(down_weight() / s[:, None]),
        "q_ln_g": bf((1.0 + 0.1 * np.random.standard_normal(LAT)) * tq),
        "q_ln_b": bf(0.1 * np.random.standard_normal(LAT) * tq),
        "W_uq": bf(np.random.standard_normal((LAT, D)) / np.sqrt(LAT) / tq[:, None]),
        "W_dkv": bf(down_weight() / s[:, None]),
        "kv_ln_g": bf((1.0 + 0.1 * np.random.standard_normal(LAT)) * tkv),
        "kv_ln_b": bf(0.1 * np.random.standard_normal(LAT) * tkv),
        "W_ukv": bf(np.random.standard_normal((LAT, D + D)) / np.sqrt(LAT) / tkv[:, None]),
    }


def reference(normed, W_dq, q_ln_g, q_ln_b, W_uq, W_dkv, kv_ln_g, kv_ln_b, W_ukv):
    nq = mxq(f64(normed), 2, "e4m3")
    cq = layer_norm(nq @ mxq(f64(W_dq), 0, "e4m3"), f64(q_ln_g), f64(q_ln_b))
    Q = mxq(cq, 2, "e4m3") @ mxq(f64(W_uq), 0, "e4m3")
    ckv = layer_norm(nq @ mxq(f64(W_dkv), 0, "e4m3"), f64(kv_ln_g), f64(kv_ln_b))
    KV = mxq(ckv, 2, "e4m3") @ mxq(f64(W_ukv), 0, "e4m3")
    return Q, KV

@@ -1,0 +1,266 @@
+from contextlib import ExitStack
+
+import concourse.mybir as mybir
+from concourse.masks import make_identity
+
+F32 = mybir.dt.float32
+BF16 = mybir.dt.bfloat16
+U32 = mybir.dt.uint32
+U8 = mybir.dt.uint8
+FP8X4 = mybir.dt.float8_e4m3fn_x4
+ALU = mybir.AluOpType
+ACT = mybir.ActivationFunctionType
+
+P = 128
+PACK = 4
+K_PASS = P * PACK
+TOKENS = 512
+D_MODEL = 2048
+LATENT = 512
+TOKEN_TILES = TOKENS // P
+DOWN_PASSES = D_MODEL // K_PASS
+N_TILE = 512
+KV_CHUNKS = 2
+EPS = 1e-5
+
+FLOPS = 2 * TOKENS * D_MODEL * LATENT * 2 + 2 * TOKENS * LATENT * (D_MODEL + 2 * D_MODEL)
+
+
+def regroup(nc, on_scalar, grouped, rows):
+    dst = grouped.rearrange("p (c i) t -> p c t i", i=4)
+    src = rows.rearrange("p t (c i) -> p c t i", i=4)
+    if on_scalar:
+        nc.scalar.copy(out=dst, in_=src)
+    else:
+        nc.vector.tensor_copy(out=dst, in_=src)
+
+
+def quantise_weight_piece(nc, stage, on_scalar, rows, codes, scales):
+    grouped = stage.tile([P, N_TILE, PACK], BF16, tag="grouped", align_bytes=64)
+    regroup(nc, on_scalar, grouped[:], rows)
+    nc.vector.quantize_mx(
+        out=codes.bitcast(FP8X4),
+        scales=scales,
+        in_=grouped[:].rearrange("p n t -> p (n t)"),
+    )
+
+
+def tile_transformerdecoderblock_pa_kernel(
+    tc, normed, W_dq, q_ln_g, q_ln_b, W_uq, W_dkv, kv_ln_g, kv_ln_b, W_ukv, out_0, out_1
+):
+    nc = tc.nc
+    with ExitStack() as ctx:
+        const = ctx.enter_context(tc.tile_pool(name="const", bufs=1))
+        raw = ctx.enter_context(tc.tile_pool(name="raw", bufs=1))
+        keep = ctx.enter_context(tc.tile_pool(name="keep", bufs=1))
+        stage = ctx.enter_context(tc.tile_pool(name="stage", bufs=4))
+        ln = ctx.enter_context(tc.tile_pool(name="ln", bufs=2))
+        small = ctx.enter_context(tc.tile_pool(name="small", bufs=4))
+        outp = ctx.enter_context(tc.tile_pool(name="outp", bufs=4))
+        psum_t = ctx.enter_context(tc.psum_pool(name="psum_t", bufs=2))
+        psum_acc = ctx.enter_context(tc.psum_pool(name="psum_acc", bufs=2))
+        psum_out = ctx.enter_context(tc.psum_pool(name="psum_out", bufs=4))
+
+        x_view = normed.flatten_outer_dims().rearrange("(p i) d -> p i d", i=TOKEN_TILES)
+        q_view = out_0.flatten_outer_dims().rearrange("(p i) n -> p i n", i=TOKEN_TILES)
+        kv_view = out_1.flatten_outer_dims().rearrange("(p i) n -> p i n", i=TOKEN_TILES)
+
+        eps = const.tile([P, 1], F32)
+        nc.vector.memset(eps[:], EPS)
+        warm = const.tile([P, 1], F32)
+        nc.scalar.activation(out=warm[:], in_=eps[:], func=ACT.Sqrt)
+        ones = const.tile([P, P], BF16)
+        nc.vector.memset(ones[:], 1.0)
+        vector_row = const.tile([P, 4 * LATENT], BF16)
+        nc.vector.memset(vector_row[:], 0.0)
+        ident_f32 = const.tile([P, P], F32)
+        make_identity(nc, ident_f32[:])
+        ident_bf16 = const.tile([P, P], BF16)
+        make_identity(nc, ident_bf16[:])
+
+        vector_in = const.tile([1, 4 * LATENT], BF16)
+        for v, vec in enumerate((q_ln_g, q_ln_b, kv_ln_g, kv_ln_b)):
+            nc.scalar.dma_start(
+                out=vector_in[0:1, v * LATENT : (v + 1) * LATENT],
+                in_=vec.rearrange("(o n) -> o n", o=1),
+            )
+        nc.vector.tensor_copy(out=vector_row[0:1, :], in_=vector_in[:])
+
+        x_raw = raw.tile([P, TOKEN_TILES, D_MODEL], BF16)
+        wdq_raw = raw.tile([P, 2 * DOWN_PASSES, 2 * LATENT], BF16)
+        wdkv_raw = raw.tile([P, 2 * DOWN_PASSES, 2 * LATENT], BF16)
+        wuq_raw = raw.tile([P, PACK, D_MODEL], BF16)
+        wukv_raw = raw.tile([P, PACK, 2 * D_MODEL], BF16)
+
+        wdq_view = W_dq.rearrange("(a p e) n -> p a (e n)", a=2 * DOWN_PASSES, p=P, e=2)
+        wdkv_view = W_dkv.rearrange("(a p e) n -> p a (e n)", a=2 * DOWN_PASSES, p=P, e=2)
+        wuq_view = W_uq.rearrange("(j p) n -> p j n", j=PACK, p=P)
+        wukv_view = W_ukv.rearrange("(j p) n -> p j n", j=PACK, p=P)
+
+        nc.sync.dma_start(out=wdq_raw[:, 0:2, :], in_=wdq_view[:, 0:2, :])
+        nc.sync.dma_start(out=wdq_raw[:, 2:4, :], in_=wdq_view[:, 2:4, :])
+        nc.sync.dma_start(out=x_raw[:, 0:1, :], in_=x_view[:, 0:1, :])
+        nc.sync.dma_start(out=wdq_raw[:, 4:6, :], in_=wdq_view[:, 4:6, :])
+        nc.sync.dma_start(out=wdq_raw[:, 6:8, :], in_=wdq_view[:, 6:8, :])
+        nc.sync.dma_start(out=x_raw[:, 1:2, :], in_=x_view[:, 1:2, :])
+        nc.sync.dma_start(out=x_raw[:, 2:4, :], in_=x_view[:, 2:4, :])
+        for half in range(2):
+            rows = slice(2 * half, 2 * half + 2)
+            nc.sync.dma_start(out=wuq_raw[:, rows, :], in_=wuq_view[:, rows, :])
+        for half in range(2):
+            rows = slice(4 * half, 4 * half + 4)
+            nc.sync.dma_start(out=wdkv_raw[:, rows, :], in_=wdkv_view[:, rows, :])
+        for j in range(PACK):
+            nc.sync.dma_start(out=wukv_raw[:, j : j + 1, :], in_=wukv_view[:, j : j + 1, :])
+
+        x_codes = keep.tile([P, TOKEN_TILES, DOWN_PASSES * P], U32, align_bytes=64)
+        x_scales = keep.tile([P, TOKEN_TILES, DOWN_PASSES * P], U8, align_bytes=64)
+        wdq_codes = keep.tile([P, DOWN_PASSES, LATENT], U32, align_bytes=64)
+        wdq_scales = keep.tile([P, DOWN_PASSES, LATENT], U8, align_bytes=64)
+        wdkv_codes = keep.tile([P, DOWN_PASSES, LATENT], U32, align_bytes=64)
+        wdkv_scales = keep.tile([P, DOWN_PASSES, LATENT], U8, align_bytes=64)
+        wuq_codes = keep.tile([P, D_MODEL // N_TILE, N_TILE], U32, align_bytes=64)
+        wuq_scales = keep.tile([P, D_MODEL // N_TILE, N_TILE], U8, align_bytes=64)
+        wukv_codes = keep.tile([P, 2 * D_MODEL // N_TILE, N_TILE], U32, align_bytes=64)
+        wukv_scales = keep.tile([P, 2 * D_MODEL // N_TILE, N_TILE], U8, align_bytes=64)
+        cq_codes = keep.tile([P, TOKEN_TILES, P], U32, align_bytes=64)
+        cq_scales = keep.tile([P, TOKEN_TILES, P], U8, align_bytes=64)
+        ckv_codes = keep.tile([P, TOKEN_TILES, P], U32, align_bytes=64)
+        ckv_scales = keep.tile([P, TOKEN_TILES, P], U8, align_bytes=64)
+
+        spread = const.tile([P, 4, LATENT], BF16)
+        for v in range(4):
+            spread_ps = psum_t.tile([P, LATENT], F32, tag="flip")
+            nc.tensor.matmul(
+                out=spread_ps[:],
+                lhsT=ones[:],
+                rhs=vector_row[:, v * LATENT : (v + 1) * LATENT],
+                start=True,
+                stop=True,
+            )
+            nc.scalar.copy(out=spread[:, v, :], in_=spread_ps[:])
+
+        def quantise_token_tile(i):
+            words = x_raw[:, i, :].bitcast(F32)
+            x_grouped = stage.tile([P, DOWN_PASSES * P * PACK], BF16, tag="grouped", align_bytes=64)
+            grouped_words = x_grouped[:].bitcast(F32).rearrange(
+                "p (g r u) -> p g r u", g=DOWN_PASSES, r=P, u=2
+            )
+            for half in range(2):
+                flipped = psum_t.tile([P, 2, 2, P], F32, tag="flip")
+                for g_local in range(2):
+                    for u in range(2):
+                        first = (2 * (2 * half + g_local) + u) * P
+                        nc.tensor.transpose(
+                            flipped[:, g_local, u, :], words[:, first : first + P], ident_f32[:]
+                        )
+                nc.scalar.copy(
+                    out=grouped_words[:, 2 * half : 2 * half + 2, :, :],
+                    in_=flipped[:].rearrange("p g u r -> p g r u"),
+                )
+            nc.vector.quantize_mx(
+                out=x_codes[:, i, :].bitcast(FP8X4), scales=x_scales[:, i, :], in_=x_grouped[:]
+            )
+
+        def quantise_down_piece(g, on_scalar, wd_raw, wd_codes, wd_scales):
+            rows = wd_raw[:, 2 * g : 2 * g + 2, :].rearrange("p u (e n) -> p (u e) n", e=2)
+            quantise_weight_piece(nc, stage, on_scalar, rows, wd_codes[:, g, :], wd_scales[:, g, :])
+
+        def quantise_up_piece(c, on_scalar, wu_raw, wu_codes, wu_scales):
+            rows = wu_raw[:, :, c * N_TILE : (c + 1) * N_TILE]
+            quantise_weight_piece(nc, stage, on_scalar, rows, wu_codes[:, c, :], wu_scales[:, c, :])
+
+        def latent_tile(i, wd_codes, wd_scales, gain, bias, c_codes, c_scales):
+            acc = psum_acc.tile([P, LATENT], F32, tag="acc")
+            for g in range(DOWN_PASSES):
+                cols = slice(g * P, (g + 1) * P)
+                nc.tensor.matmul_mx(
+                    out=acc[:],
+                    lhsT=x_codes[:, i, cols].bitcast(FP8X4),
+                    lhsT_scale=x_scales[:, i, cols],
+                    rhs=wd_codes[:, g, :].bitcast(FP8X4),
+                    rhs_scale=wd_scales[:, g, :],
+                    start=(g == 0),
+                    stop=(g == DOWN_PASSES - 1),
+                )
+            stats = small.tile([P, 6], F32, tag="stats")
+            nc.vector.bn_stats(out=stats[:], in_=acc[:])
+            mean_var = small.tile([P, 2], F32, tag="mean_var")
+            nc.vector.bn_aggr(out=mean_var[:], in_=stats[:])
+            centred = ln.tile([P, LATENT], F32, tag="centred")
+            nc.vector.scalar_tensor_tensor(
+                out=centred[:], in0=acc[:], scalar=mean_var[:, 0:1], in1=gain,
+                op0=ALU.subtract, op1=ALU.mult,
+            )
+            std = small.tile([P, 1], F32, tag="std")
+            nc.scalar.activation(out=std[:], in_=mean_var[:, 1:2], func=ACT.Sqrt, bias=eps[:], scale=1.0)
+            rstd = small.tile([P, 1], F32, tag="rstd")
+            nc.vector.reciprocal(out=rstd[:], in_=std[:])
+            latent = ln.tile([P, LATENT], BF16, tag="latent")
+            nc.vector.scalar_tensor_tensor(
+                out=latent[:], in0=centred[:], scalar=rstd[:], in1=bias,
+                op0=ALU.mult, op1=ALU.add,
+            )
+            flipped = psum_t.tile([P, PACK, P], BF16, tag="flip")
+            for j in range(PACK):
+                nc.tensor.transpose(flipped[:, j, :], latent[:, j * P : (j + 1) * P], ident_bf16[:])
+            c_grouped = stage.tile([P, P, PACK], BF16, tag="c_grouped", bufs=2, align_bytes=64)
+            nc.scalar.copy(out=c_grouped[:], in_=flipped[:].rearrange("p j r -> p r j"))
+            nc.vector.quantize_mx(
+                out=c_codes[:, i, :].bitcast(FP8X4),
+                scales=c_scales[:, i, :],
+                in_=c_grouped[:].rearrange("p r j -> p (r j)"),
+            )
+
+        def project_up(i, first_chunk, chunks, vector_share, c_codes, c_scales, wu_codes, wu_scales, out_view):
+            staging = outp.tile([P, chunks * N_TILE], F32, tag="staging")
+            for h in range(chunks):
+                chunk = first_chunk + h
+                bank = psum_out.tile([P, N_TILE], F32, tag="bank")
+                nc.tensor.matmul_mx(
+                    out=bank[:],
+                    lhsT=c_codes[:, i, :].bitcast(FP8X4),
+                    lhsT_scale=c_scales[:, i, :],
+                    rhs=wu_codes[:, chunk, :].bitcast(FP8X4),
+                    rhs_scale=wu_scales[:, chunk, :],
+                    start=True,
+                    stop=True,
+                )
+                dst = staging[:, h * N_TILE : (h + 1) * N_TILE]
+                if vector_share and h % 2 == 1:
+                    nc.vector.tensor_copy(out=dst, in_=bank[:])
+                else:
+                    nc.scalar.copy(out=dst, in_=bank[:])
+            first_col = first_chunk * N_TILE
+            nc.sync.dma_start(
+                out=out_view[:, i, first_col : first_col + chunks * N_TILE], in_=staging[:]
+            )
+
+        quantise_down_piece(0, False, wdq_raw, wdq_codes, wdq_scales)
+        quantise_down_piece(1, False, wdq_raw, wdq_codes, wdq_scales)
+        quantise_token_tile(0)
+        quantise_down_piece(2, False, wdq_raw, wdq_codes, wdq_scales)
+        quantise_down_piece(3, True, wdq_raw, wdq_codes, wdq_scales)
+        quantise_token_tile(1)
+        for i in range(TOKEN_TILES):
+            if i + 2 < TOKEN_TILES:
+                quantise_token_tile(i + 2)
+            latent_tile(i, wdq_codes, wdq_scales, spread[:, 0, :], spread[:, 1, :], cq_codes, cq_scales)
+        for c in range(D_MODEL // N_TILE):
+            quantise_up_piece(c, c % 2 == 1, wuq_raw, wuq_codes, wuq_scales)
+        for g in range(DOWN_PASSES):
+            quantise_down_piece(g, g < DOWN_PASSES - 1, wdkv_raw, wdkv_codes, wdkv_scales)
+        for i in range(TOKEN_TILES):
+            latent_tile(i, wdkv_codes, wdkv_scales, spread[:, 2, :], spread[:, 3, :], ckv_codes, ckv_scales)
+        for i in range(TOKEN_TILES):
+            project_up(i, 0, D_MODEL // N_TILE, False, cq_codes, cq_scales, wuq_codes, wuq_scales, q_view)
+        kv_groups = 2 * D_MODEL // (KV_CHUNKS * N_TILE)
+        for group in range(kv_groups):
+            first_chunk = group * KV_CHUNKS
+            for c in range(first_chunk, first_chunk + KV_CHUNKS):
+                quantise_up_piece(c, False, wukv_raw, wukv_codes, wukv_scales)
+            for i in range(TOKEN_TILES):
+                project_up(
+                    i, first_chunk, KV_CHUNKS, group >= kv_groups // 2,
+                    ckv_codes, ckv_scales, wukv_codes, wukv_scales, kv_view,
+                )

@@ -20,7 +20,7 @@ LATENT = 512
 TOKEN_TILES = TOKENS // P
 DOWN_PASSES = D_MODEL // K_PASS
 N_TILE = 512
-KV_CHUNKS = 2
+STORE_CHUNKS = 2
 EPS = 1e-5
 
 FLOPS = 2 * TOKENS * D_MODEL * LATENT * 2 + 2 * TOKENS * LATENT * (D_MODEL + 2 * D_MODEL)
@@ -53,13 +53,13 @@ def tile_transformerdecoderblock_pa_kernel(
         const = ctx.enter_context(tc.tile_pool(name="const", bufs=1))
         raw = ctx.enter_context(tc.tile_pool(name="raw", bufs=1))
         keep = ctx.enter_context(tc.tile_pool(name="keep", bufs=1))
-        stage = ctx.enter_context(tc.tile_pool(name="stage", bufs=4))
+        stage = ctx.enter_context(tc.tile_pool(name="stage", bufs=6))
         ln = ctx.enter_context(tc.tile_pool(name="ln", bufs=2))
         small = ctx.enter_context(tc.tile_pool(name="small", bufs=4))
-        outp = ctx.enter_context(tc.tile_pool(name="outp", bufs=4))
-        psum_t = ctx.enter_context(tc.psum_pool(name="psum_t", bufs=2))
+        outp = ctx.enter_context(tc.tile_pool(name="outp", bufs=6))
+        psum_t = ctx.enter_context(tc.psum_pool(name="psum_t", bufs=3))
         psum_acc = ctx.enter_context(tc.psum_pool(name="psum_acc", bufs=2))
-        psum_out = ctx.enter_context(tc.psum_pool(name="psum_out", bufs=4))
+        psum_out = ctx.enter_context(tc.psum_pool(name="psum_out", bufs=3))
 
         x_view = normed.flatten_outer_dims().rearrange("(p i) d -> p i d", i=TOKEN_TILES)
         q_view = out_0.flatten_outer_dims().rearrange("(p i) n -> p i n", i=TOKEN_TILES)
@@ -78,14 +78,6 @@ def tile_transformerdecoderblock_pa_kernel(
         ident_bf16 = const.tile([P, P], BF16)
         make_identity(nc, ident_bf16[:])
 
-        vector_in = const.tile([1, 4 * LATENT], BF16)
-        for v, vec in enumerate((q_ln_g, q_ln_b, kv_ln_g, kv_ln_b)):
-            nc.scalar.dma_start(
-                out=vector_in[0:1, v * LATENT : (v + 1) * LATENT],
-                in_=vec.rearrange("(o n) -> o n", o=1),
-            )
-        nc.vector.tensor_copy(out=vector_row[0:1, :], in_=vector_in[:])
-
         x_raw = raw.tile([P, TOKEN_TILES, D_MODEL], BF16)
         wdq_raw = raw.tile([P, 2 * DOWN_PASSES, 2 * LATENT], BF16)
         wdkv_raw = raw.tile([P, 2 * DOWN_PASSES, 2 * LATENT], BF16)
@@ -98,8 +90,15 @@ def tile_transformerdecoderblock_pa_kernel(
         wukv_view = W_ukv.rearrange("(j p) n -> p j n", j=PACK, p=P)
 
         nc.sync.dma_start(out=wdq_raw[:, 0:2, :], in_=wdq_view[:, 0:2, :])
-        nc.sync.dma_start(out=wdq_raw[:, 2:4, :], in_=wdq_view[:, 2:4, :])
         nc.sync.dma_start(out=x_raw[:, 0:1, :], in_=x_view[:, 0:1, :])
+        vector_in = const.tile([1, 4 * LATENT], BF16)
+        for v, vec in enumerate((q_ln_g, q_ln_b, kv_ln_g, kv_ln_b)):
+            nc.sync.dma_start(
+                out=vector_in[0:1, v * LATENT : (v + 1) * LATENT],
+                in_=vec.rearrange("(o n) -> o n", o=1),
+            )
+        nc.vector.tensor_copy(out=vector_row[0:1, :], in_=vector_in[:])
+        nc.sync.dma_start(out=wdq_raw[:, 2:4, :], in_=wdq_view[:, 2:4, :])
         nc.sync.dma_start(out=wdq_raw[:, 4:6, :], in_=wdq_view[:, 4:6, :])
         nc.sync.dma_start(out=wdq_raw[:, 6:8, :], in_=wdq_view[:, 6:8, :])
         nc.sync.dma_start(out=x_raw[:, 1:2, :], in_=x_view[:, 1:2, :])
@@ -240,27 +239,31 @@ def tile_transformerdecoderblock_pa_kernel(
         quantise_down_piece(1, False, wdq_raw, wdq_codes, wdq_scales)
         quantise_token_tile(0)
         quantise_down_piece(2, False, wdq_raw, wdq_codes, wdq_scales)
-        quantise_down_piece(3, True, wdq_raw, wdq_codes, wdq_scales)
+        quantise_down_piece(3, False, wdq_raw, wdq_codes, wdq_scales)
         quantise_token_tile(1)
         for i in range(TOKEN_TILES):
             if i + 2 < TOKEN_TILES:
                 quantise_token_tile(i + 2)
             latent_tile(i, wdq_codes, wdq_scales, spread[:, 0, :], spread[:, 1, :], cq_codes, cq_scales)
         for c in range(D_MODEL // N_TILE):
-            quantise_up_piece(c, c % 2 == 1, wuq_raw, wuq_codes, wuq_scales)
+            quantise_up_piece(c, c == 1, wuq_raw, wuq_codes, wuq_scales)
         for g in range(DOWN_PASSES):
-            quantise_down_piece(g, g < DOWN_PASSES - 1, wdkv_raw, wdkv_codes, wdkv_scales)
+            quantise_down_piece(g, True, wdkv_raw, wdkv_codes, wdkv_scales)
         for i in range(TOKEN_TILES):
             latent_tile(i, wdkv_codes, wdkv_scales, spread[:, 2, :], spread[:, 3, :], ckv_codes, ckv_scales)
         for i in range(TOKEN_TILES):
-            project_up(i, 0, D_MODEL // N_TILE, False, cq_codes, cq_scales, wuq_codes, wuq_scales, q_view)
-        kv_groups = 2 * D_MODEL // (KV_CHUNKS * N_TILE)
+            for first_chunk in range(0, D_MODEL // N_TILE, STORE_CHUNKS):
+                project_up(
+                    i, first_chunk, STORE_CHUNKS, False,
+                    cq_codes, cq_scales, wuq_codes, wuq_scales, q_view,
+                )
+        kv_groups = 2 * D_MODEL // (STORE_CHUNKS * N_TILE)
         for group in range(kv_groups):
-            first_chunk = group * KV_CHUNKS
-            for c in range(first_chunk, first_chunk + KV_CHUNKS):
+            first_chunk = group * STORE_CHUNKS
+            for c in range(first_chunk, first_chunk + STORE_CHUNKS):
                 quantise_up_piece(c, False, wukv_raw, wukv_codes, wukv_scales)
             for i in range(TOKEN_TILES):
                 project_up(
-                    i, first_chunk, KV_CHUNKS, group >= kv_groups // 2,
+                    i, first_chunk, STORE_CHUNKS, group == kv_groups - 1,
                     ckv_codes, ckv_scales, wukv_codes, wukv_scales, kv_view,
                 )

@@ -26,23 +26,33 @@ EPS = 1e-5
 FLOPS = 2 * TOKENS * D_MODEL * LATENT * 2 + 2 * TOKENS * LATENT * (D_MODEL + 2 * D_MODEL)
 
 
-def regroup(nc, on_scalar, grouped, rows):
-    dst = grouped.rearrange("p (c i) t -> p c t i", i=4)
+def regroup(nc, stage, on_scalar, rows):
+    grouped = stage.tile([P, N_TILE, PACK], BF16, tag="grouped", align_bytes=64)
+    dst = grouped[:].rearrange("p (c i) t -> p c t i", i=4)
     src = rows.rearrange("p t (c i) -> p c t i", i=4)
     if on_scalar:
         nc.scalar.copy(out=dst, in_=src)
     else:
         nc.vector.tensor_copy(out=dst, in_=src)
+    return grouped
 
 
-def quantise_weight_piece(nc, stage, on_scalar, rows, codes, scales):
-    grouped = stage.tile([P, N_TILE, PACK], BF16, tag="grouped", align_bytes=64)
-    regroup(nc, on_scalar, grouped[:], rows)
+def quantise(nc, grouped, codes, scales):
     nc.vector.quantize_mx(
         out=codes.bitcast(FP8X4),
         scales=scales,
         in_=grouped[:].rearrange("p n t -> p (n t)"),
     )
+
+
+def quantise_pieces(nc, stage, pieces):
+    waiting = None
+    for on_scalar, rows, codes, scales in pieces:
+        grouped = regroup(nc, stage, on_scalar, rows)
+        if waiting is not None:
+            quantise(nc, waiting[0], waiting[1], waiting[2])
+        waiting = (grouped, codes, scales)
+    quantise(nc, waiting[0], waiting[1], waiting[2])
 
 
 def tile_transformerdecoderblock_pa_kernel(
@@ -54,7 +64,7 @@ def tile_transformerdecoderblock_pa_kernel(
         raw = ctx.enter_context(tc.tile_pool(name="raw", bufs=1))
         keep = ctx.enter_context(tc.tile_pool(name="keep", bufs=1))
         stage = ctx.enter_context(tc.tile_pool(name="stage", bufs=6))
-        ln = ctx.enter_context(tc.tile_pool(name="ln", bufs=2))
+        ln = ctx.enter_context(tc.tile_pool(name="ln", bufs=4))
         small = ctx.enter_context(tc.tile_pool(name="small", bufs=4))
         outp = ctx.enter_context(tc.tile_pool(name="outp", bufs=6))
         psum_t = ctx.enter_context(tc.psum_pool(name="psum_t", bufs=3))
@@ -71,8 +81,6 @@ def tile_transformerdecoderblock_pa_kernel(
         nc.scalar.activation(out=warm[:], in_=eps[:], func=ACT.Sqrt)
         ones = const.tile([P, P], BF16)
         nc.vector.memset(ones[:], 1.0)
-        vector_row = const.tile([P, 4 * LATENT], BF16)
-        nc.vector.memset(vector_row[:], 0.0)
         ident_f32 = const.tile([P, P], F32)
         make_identity(nc, ident_f32[:])
         ident_bf16 = const.tile([P, P], BF16)
@@ -91,13 +99,12 @@ def tile_transformerdecoderblock_pa_kernel(
 
         nc.sync.dma_start(out=wdq_raw[:, 0:2, :], in_=wdq_view[:, 0:2, :])
         nc.sync.dma_start(out=x_raw[:, 0:1, :], in_=x_view[:, 0:1, :])
-        vector_in = const.tile([1, 4 * LATENT], BF16)
+        vector_in = stage.tile([1, 4 * LATENT], BF16, tag="grouped", align_bytes=64)
         for v, vec in enumerate((q_ln_g, q_ln_b, kv_ln_g, kv_ln_b)):
             nc.sync.dma_start(
                 out=vector_in[0:1, v * LATENT : (v + 1) * LATENT],
                 in_=vec.rearrange("(o n) -> o n", o=1),
             )
-        nc.vector.tensor_copy(out=vector_row[0:1, :], in_=vector_in[:])
         nc.sync.dma_start(out=wdq_raw[:, 2:4, :], in_=wdq_view[:, 2:4, :])
         nc.sync.dma_start(out=wdq_raw[:, 4:6, :], in_=wdq_view[:, 4:6, :])
         nc.sync.dma_start(out=wdq_raw[:, 6:8, :], in_=wdq_view[:, 6:8, :])
@@ -127,6 +134,9 @@ def tile_transformerdecoderblock_pa_kernel(
         ckv_codes = keep.tile([P, TOKEN_TILES, P], U32, align_bytes=64)
         ckv_scales = keep.tile([P, TOKEN_TILES, P], U8, align_bytes=64)
 
+        vector_row = stage.tile([P, 4 * LATENT], BF16, tag="grouped", align_bytes=64)
+        nc.vector.memset(vector_row[:], 0.0)
+        nc.vector.tensor_copy(out=vector_row[0:1, :], in_=vector_in[:])
         spread = const.tile([P, 4, LATENT], BF16)
         for v in range(4):
             spread_ps = psum_t.tile([P, LATENT], F32, tag="flip")
@@ -161,55 +171,80 @@ def tile_transformerdecoderblock_pa_kernel(
                 out=x_codes[:, i, :].bitcast(FP8X4), scales=x_scales[:, i, :], in_=x_grouped[:]
             )
 
-        def quantise_down_piece(g, on_scalar, wd_raw, wd_codes, wd_scales):
+        def down_piece(g, on_scalar, wd_raw, wd_codes, wd_scales):
             rows = wd_raw[:, 2 * g : 2 * g + 2, :].rearrange("p u (e n) -> p (u e) n", e=2)
-            quantise_weight_piece(nc, stage, on_scalar, rows, wd_codes[:, g, :], wd_scales[:, g, :])
+            return (on_scalar, rows, wd_codes[:, g, :], wd_scales[:, g, :])
 
-        def quantise_up_piece(c, on_scalar, wu_raw, wu_codes, wu_scales):
+        def up_piece(c, on_scalar, wu_raw, wu_codes, wu_scales):
             rows = wu_raw[:, :, c * N_TILE : (c + 1) * N_TILE]
-            quantise_weight_piece(nc, stage, on_scalar, rows, wu_codes[:, c, :], wu_scales[:, c, :])
+            return (on_scalar, rows, wu_codes[:, c, :], wu_scales[:, c, :])
 
-        def latent_tile(i, wd_codes, wd_scales, gain, bias, c_codes, c_scales):
-            acc = psum_acc.tile([P, LATENT], F32, tag="acc")
-            for g in range(DOWN_PASSES):
-                cols = slice(g * P, (g + 1) * P)
-                nc.tensor.matmul_mx(
-                    out=acc[:],
-                    lhsT=x_codes[:, i, cols].bitcast(FP8X4),
-                    lhsT_scale=x_scales[:, i, cols],
-                    rhs=wd_codes[:, g, :].bitcast(FP8X4),
-                    rhs_scale=wd_scales[:, g, :],
-                    start=(g == 0),
-                    stop=(g == DOWN_PASSES - 1),
+        def latent_tiles(tiles, wd_codes, wd_scales, gain, bias, c_codes, c_scales):
+            accs = {}
+            for i in tiles:
+                acc = psum_acc.tile([P, LATENT], F32, tag="acc")
+                for g in range(DOWN_PASSES):
+                    cols = slice(g * P, (g + 1) * P)
+                    nc.tensor.matmul_mx(
+                        out=acc[:],
+                        lhsT=x_codes[:, i, cols].bitcast(FP8X4),
+                        lhsT_scale=x_scales[:, i, cols],
+                        rhs=wd_codes[:, g, :].bitcast(FP8X4),
+                        rhs_scale=wd_scales[:, g, :],
+                        start=(g == 0),
+                        stop=(g == DOWN_PASSES - 1),
+                    )
+                accs[i] = acc
+            all_stats = {}
+            for i in tiles:
+                stats = small.tile([P, 6], F32, tag="stats")
+                nc.vector.bn_stats(out=stats[:], in_=accs[i][:])
+                all_stats[i] = stats
+            means = {}
+            for i in tiles:
+                mean_var = small.tile([P, 2], F32, tag="mean_var")
+                nc.vector.bn_aggr(out=mean_var[:], in_=all_stats[i][:])
+                means[i] = mean_var
+            stds = {}
+            for i in tiles:
+                std = small.tile([P, 1], F32, tag="std")
+                nc.scalar.activation(
+                    out=std[:], in_=means[i][:, 1:2], func=ACT.Sqrt, bias=eps[:], scale=1.0
                 )
-            stats = small.tile([P, 6], F32, tag="stats")
-            nc.vector.bn_stats(out=stats[:], in_=acc[:])
-            mean_var = small.tile([P, 2], F32, tag="mean_var")
-            nc.vector.bn_aggr(out=mean_var[:], in_=stats[:])
-            centred = ln.tile([P, LATENT], F32, tag="centred")
-            nc.vector.scalar_tensor_tensor(
-                out=centred[:], in0=acc[:], scalar=mean_var[:, 0:1], in1=gain,
-                op0=ALU.subtract, op1=ALU.mult,
-            )
-            std = small.tile([P, 1], F32, tag="std")
-            nc.scalar.activation(out=std[:], in_=mean_var[:, 1:2], func=ACT.Sqrt, bias=eps[:], scale=1.0)
-            rstd = small.tile([P, 1], F32, tag="rstd")
-            nc.vector.reciprocal(out=rstd[:], in_=std[:])
-            latent = ln.tile([P, LATENT], BF16, tag="latent")
-            nc.vector.scalar_tensor_tensor(
-                out=latent[:], in0=centred[:], scalar=rstd[:], in1=bias,
-                op0=ALU.mult, op1=ALU.add,
-            )
-            flipped = psum_t.tile([P, PACK, P], BF16, tag="flip")
-            for j in range(PACK):
-                nc.tensor.transpose(flipped[:, j, :], latent[:, j * P : (j + 1) * P], ident_bf16[:])
-            c_grouped = stage.tile([P, P, PACK], BF16, tag="c_grouped", bufs=2, align_bytes=64)
-            nc.scalar.copy(out=c_grouped[:], in_=flipped[:].rearrange("p j r -> p r j"))
-            nc.vector.quantize_mx(
-                out=c_codes[:, i, :].bitcast(FP8X4),
-                scales=c_scales[:, i, :],
-                in_=c_grouped[:].rearrange("p r j -> p (r j)"),
-            )
+                stds[i] = std
+            centreds = {}
+            for i in tiles:
+                centred = ln.tile([P, LATENT], F32, tag="centred")
+                nc.vector.scalar_tensor_tensor(
+                    out=centred[:], in0=accs[i][:], scalar=means[i][:, 0:1], in1=gain,
+                    op0=ALU.subtract, op1=ALU.mult,
+                )
+                centreds[i] = centred
+            rstds = {}
+            for i in tiles:
+                rstd = small.tile([P, 1], F32, tag="rstd")
+                nc.vector.reciprocal(out=rstd[:], in_=stds[i][:])
+                rstds[i] = rstd
+            latents = {}
+            for i in tiles:
+                latent = ln.tile([P, LATENT], BF16, tag="latent")
+                nc.vector.scalar_tensor_tensor(
+                    out=latent[:], in0=centreds[i][:], scalar=rstds[i][:], in1=bias,
+                    op0=ALU.mult, op1=ALU.add,
+                )
+                latents[i] = latent
+            groupeds = {}
+            for i in tiles:
+                flipped = psum_t.tile([P, PACK, P], BF16, tag="flip")
+                for j in range(PACK):
+                    nc.tensor.transpose(
+                        flipped[:, j, :], latents[i][:, j * P : (j + 1) * P], ident_bf16[:]
+                    )
+                c_grouped = stage.tile([P, P, PACK], BF16, tag="c_grouped", bufs=4, align_bytes=64)
+                nc.scalar.copy(out=c_grouped[:], in_=flipped[:].rearrange("p j r -> p r j"))
+                groupeds[i] = c_grouped
+            for i in tiles:
+                quantise(nc, groupeds[i], c_codes[:, i, :], c_scales[:, i, :])
 
         def project_up(i, first_chunk, chunks, vector_share, c_codes, c_scales, wu_codes, wu_scales, out_view):
             staging = outp.tile([P, chunks * N_TILE], F32, tag="staging")
@@ -235,35 +270,45 @@ def tile_transformerdecoderblock_pa_kernel(
                 out=out_view[:, i, first_col : first_col + chunks * N_TILE], in_=staging[:]
             )
 
-        quantise_down_piece(0, False, wdq_raw, wdq_codes, wdq_scales)
-        quantise_down_piece(1, False, wdq_raw, wdq_codes, wdq_scales)
         quantise_token_tile(0)
-        quantise_down_piece(2, False, wdq_raw, wdq_codes, wdq_scales)
-        quantise_down_piece(3, False, wdq_raw, wdq_codes, wdq_scales)
-        quantise_token_tile(1)
-        for i in range(TOKEN_TILES):
-            if i + 2 < TOKEN_TILES:
-                quantise_token_tile(i + 2)
-            latent_tile(i, wdq_codes, wdq_scales, spread[:, 0, :], spread[:, 1, :], cq_codes, cq_scales)
-        for c in range(D_MODEL // N_TILE):
-            quantise_up_piece(c, c == 1, wuq_raw, wuq_codes, wuq_scales)
-        for g in range(DOWN_PASSES):
-            quantise_down_piece(g, True, wdkv_raw, wdkv_codes, wdkv_scales)
-        for i in range(TOKEN_TILES):
-            latent_tile(i, wdkv_codes, wdkv_scales, spread[:, 2, :], spread[:, 3, :], ckv_codes, ckv_scales)
+        quantise_pieces(
+            nc, stage, [down_piece(g, False, wdq_raw, wdq_codes, wdq_scales) for g in range(DOWN_PASSES)]
+        )
+        for i in range(1, TOKEN_TILES):
+            quantise_token_tile(i)
+        for tiles in ((0, 1), (2, 3)):
+            latent_tiles(
+                tiles, wdq_codes, wdq_scales, spread[:, 0, :], spread[:, 1, :], cq_codes, cq_scales
+            )
+        quantise_pieces(
+            nc, stage,
+            [up_piece(c, c == 1, wuq_raw, wuq_codes, wuq_scales) for c in range(D_MODEL // N_TILE)],
+        )
+        quantise_pieces(
+            nc, stage, [down_piece(g, True, wdkv_raw, wdkv_codes, wdkv_scales) for g in range(DOWN_PASSES)]
+        )
+        for tiles in ((0, 1), (2, 3)):
+            latent_tiles(
+                tiles, wdkv_codes, wdkv_scales, spread[:, 2, :], spread[:, 3, :], ckv_codes, ckv_scales
+            )
         for i in range(TOKEN_TILES):
             for first_chunk in range(0, D_MODEL // N_TILE, STORE_CHUNKS):
                 project_up(
                     i, first_chunk, STORE_CHUNKS, False,
                     cq_codes, cq_scales, wuq_codes, wuq_scales, q_view,
                 )
-        kv_groups = 2 * D_MODEL // (STORE_CHUNKS * N_TILE)
-        for group in range(kv_groups):
-            first_chunk = group * STORE_CHUNKS
+        kv_chunks = 2 * D_MODEL // N_TILE
+        kv_pieces = [up_piece(c, False, wukv_raw, wukv_codes, wukv_scales) for c in range(kv_chunks)]
+        kv_grouped = {}
+        for c in range(STORE_CHUNKS):
+            kv_grouped[c] = regroup(nc, stage, False, kv_pieces[c][1])
+        for first_chunk in range(0, kv_chunks, STORE_CHUNKS):
             for c in range(first_chunk, first_chunk + STORE_CHUNKS):
-                quantise_up_piece(c, False, wukv_raw, wukv_codes, wukv_scales)
+                quantise(nc, kv_grouped[c], kv_pieces[c][2], kv_pieces[c][3])
+                if c + STORE_CHUNKS < kv_chunks:
+                    kv_grouped[c + STORE_CHUNKS] = regroup(nc, stage, False, kv_pieces[c + STORE_CHUNKS][1])
             for i in range(TOKEN_TILES):
                 project_up(
-                    i, first_chunk, STORE_CHUNKS, group == kv_groups - 1,
+                    i, first_chunk, STORE_CHUNKS, first_chunk + STORE_CHUNKS == kv_chunks,
                     ckv_codes, ckv_scales, wukv_codes, wukv_scales, kv_view,
                 )

@@ -26,33 +26,23 @@ EPS = 1e-5
 FLOPS = 2 * TOKENS * D_MODEL * LATENT * 2 + 2 * TOKENS * LATENT * (D_MODEL + 2 * D_MODEL)
 
 
-def regroup(nc, stage, on_scalar, rows):
-    grouped = stage.tile([P, N_TILE, PACK], BF16, tag="grouped", align_bytes=64)
-    dst = grouped[:].rearrange("p (c i) t -> p c t i", i=4)
+def regroup(nc, on_scalar, grouped, rows):
+    dst = grouped.rearrange("p (c i) t -> p c t i", i=4)
     src = rows.rearrange("p t (c i) -> p c t i", i=4)
     if on_scalar:
         nc.scalar.copy(out=dst, in_=src)
     else:
         nc.vector.tensor_copy(out=dst, in_=src)
-    return grouped
 
 
-def quantise(nc, grouped, codes, scales):
+def quantise_weight_piece(nc, stage, on_scalar, rows, codes, scales):
+    grouped = stage.tile([P, N_TILE, PACK], BF16, tag="grouped", align_bytes=64)
+    regroup(nc, on_scalar, grouped[:], rows)
     nc.vector.quantize_mx(
         out=codes.bitcast(FP8X4),
         scales=scales,
         in_=grouped[:].rearrange("p n t -> p (n t)"),
     )
-
-
-def quantise_pieces(nc, stage, pieces):
-    waiting = None
-    for on_scalar, rows, codes, scales in pieces:
-        grouped = regroup(nc, stage, on_scalar, rows)
-        if waiting is not None:
-            quantise(nc, waiting[0], waiting[1], waiting[2])
-        waiting = (grouped, codes, scales)
-    quantise(nc, waiting[0], waiting[1], waiting[2])
 
 
 def tile_transformerdecoderblock_pa_kernel(
@@ -64,7 +54,7 @@ def tile_transformerdecoderblock_pa_kernel(
         raw = ctx.enter_context(tc.tile_pool(name="raw", bufs=1))
         keep = ctx.enter_context(tc.tile_pool(name="keep", bufs=1))
         stage = ctx.enter_context(tc.tile_pool(name="stage", bufs=6))
-        ln = ctx.enter_context(tc.tile_pool(name="ln", bufs=4))
+        ln = ctx.enter_context(tc.tile_pool(name="ln", bufs=2))
         small = ctx.enter_context(tc.tile_pool(name="small", bufs=4))
         outp = ctx.enter_context(tc.tile_pool(name="outp", bufs=6))
         psum_t = ctx.enter_context(tc.psum_pool(name="psum_t", bufs=3))
@@ -81,6 +71,8 @@ def tile_transformerdecoderblock_pa_kernel(
         nc.scalar.activation(out=warm[:], in_=eps[:], func=ACT.Sqrt)
         ones = const.tile([P, P], BF16)
         nc.vector.memset(ones[:], 1.0)
+        vector_row = const.tile([P, 4 * LATENT], BF16)
+        nc.vector.memset(vector_row[:], 0.0)
         ident_f32 = const.tile([P, P], F32)
         make_identity(nc, ident_f32[:])
         ident_bf16 = const.tile([P, P], BF16)
@@ -99,23 +91,24 @@ def tile_transformerdecoderblock_pa_kernel(
 
         nc.sync.dma_start(out=wdq_raw[:, 0:2, :], in_=wdq_view[:, 0:2, :])
         nc.sync.dma_start(out=x_raw[:, 0:1, :], in_=x_view[:, 0:1, :])
-        vector_in = stage.tile([1, 4 * LATENT], BF16, tag="grouped", align_bytes=64)
+        vector_in = const.tile([1, 4 * LATENT], BF16)
         for v, vec in enumerate((q_ln_g, q_ln_b, kv_ln_g, kv_ln_b)):
             nc.sync.dma_start(
                 out=vector_in[0:1, v * LATENT : (v + 1) * LATENT],
                 in_=vec.rearrange("(o n) -> o n", o=1),
             )
+        nc.vector.tensor_copy(out=vector_row[0:1, :], in_=vector_in[:])
         nc.sync.dma_start(out=wdq_raw[:, 2:4, :], in_=wdq_view[:, 2:4, :])
         nc.sync.dma_start(out=wdq_raw[:, 4:6, :], in_=wdq_view[:, 4:6, :])
         nc.sync.dma_start(out=wdq_raw[:, 6:8, :], in_=wdq_view[:, 6:8, :])
         nc.sync.dma_start(out=x_raw[:, 1:2, :], in_=x_view[:, 1:2, :])
         nc.sync.dma_start(out=x_raw[:, 2:4, :], in_=x_view[:, 2:4, :])
         for half in range(2):
-            rows = slice(2 * half, 2 * half + 2)
-            nc.sync.dma_start(out=wuq_raw[:, rows, :], in_=wuq_view[:, rows, :])
-        for half in range(2):
             rows = slice(4 * half, 4 * half + 4)
             nc.sync.dma_start(out=wdkv_raw[:, rows, :], in_=wdkv_view[:, rows, :])
+        for half in range(2):
+            rows = slice(2 * half, 2 * half + 2)
+            nc.sync.dma_start(out=wuq_raw[:, rows, :], in_=wuq_view[:, rows, :])
         for j in range(PACK):
             nc.sync.dma_start(out=wukv_raw[:, j : j + 1, :], in_=wukv_view[:, j : j + 1, :])
 
@@ -134,9 +127,6 @@ def tile_transformerdecoderblock_pa_kernel(
         ckv_codes = keep.tile([P, TOKEN_TILES, P], U32, align_bytes=64)
         ckv_scales = keep.tile([P, TOKEN_TILES, P], U8, align_bytes=64)
 
-        vector_row = stage.tile([P, 4 * LATENT], BF16, tag="grouped", align_bytes=64)
-        nc.vector.memset(vector_row[:], 0.0)
-        nc.vector.tensor_copy(out=vector_row[0:1, :], in_=vector_in[:])
         spread = const.tile([P, 4, LATENT], BF16)
         for v in range(4):
             spread_ps = psum_t.tile([P, LATENT], F32, tag="flip")
@@ -171,80 +161,55 @@ def tile_transformerdecoderblock_pa_kernel(
                 out=x_codes[:, i, :].bitcast(FP8X4), scales=x_scales[:, i, :], in_=x_grouped[:]
             )
 
-        def down_piece(g, on_scalar, wd_raw, wd_codes, wd_scales):
+        def quantise_down_piece(g, on_scalar, wd_raw, wd_codes, wd_scales):
             rows = wd_raw[:, 2 * g : 2 * g + 2, :].rearrange("p u (e n) -> p (u e) n", e=2)
-            return (on_scalar, rows, wd_codes[:, g, :], wd_scales[:, g, :])
+            quantise_weight_piece(nc, stage, on_scalar, rows, wd_codes[:, g, :], wd_scales[:, g, :])
 
-        def up_piece(c, on_scalar, wu_raw, wu_codes, wu_scales):
+        def quantise_up_piece(c, on_scalar, wu_raw, wu_codes, wu_scales):
             rows = wu_raw[:, :, c * N_TILE : (c + 1) * N_TILE]
-            return (on_scalar, rows, wu_codes[:, c, :], wu_scales[:, c, :])
+            quantise_weight_piece(nc, stage, on_scalar, rows, wu_codes[:, c, :], wu_scales[:, c, :])
 
-        def latent_tiles(tiles, wd_codes, wd_scales, gain, bias, c_codes, c_scales):
-            accs = {}
-            for i in tiles:
-                acc = psum_acc.tile([P, LATENT], F32, tag="acc")
-                for g in range(DOWN_PASSES):
-                    cols = slice(g * P, (g + 1) * P)
-                    nc.tensor.matmul_mx(
-                        out=acc[:],
-                        lhsT=x_codes[:, i, cols].bitcast(FP8X4),
-                        lhsT_scale=x_scales[:, i, cols],
-                        rhs=wd_codes[:, g, :].bitcast(FP8X4),
-                        rhs_scale=wd_scales[:, g, :],
-                        start=(g == 0),
-                        stop=(g == DOWN_PASSES - 1),
-                    )
-                accs[i] = acc
-            all_stats = {}
-            for i in tiles:
-                stats = small.tile([P, 6], F32, tag="stats")
-                nc.vector.bn_stats(out=stats[:], in_=accs[i][:])
-                all_stats[i] = stats
-            means = {}
-            for i in tiles:
-                mean_var = small.tile([P, 2], F32, tag="mean_var")
-                nc.vector.bn_aggr(out=mean_var[:], in_=all_stats[i][:])
-                means[i] = mean_var
-            stds = {}
-            for i in tiles:
-                std = small.tile([P, 1], F32, tag="std")
-                nc.scalar.activation(
-                    out=std[:], in_=means[i][:, 1:2], func=ACT.Sqrt, bias=eps[:], scale=1.0
+        def latent_tile(i, wd_codes, wd_scales, gain, bias, c_codes, c_scales):
+            acc = psum_acc.tile([P, LATENT], F32, tag="acc")
+            for g in range(DOWN_PASSES):
+                cols = slice(g * P, (g + 1) * P)
+                nc.tensor.matmul_mx(
+                    out=acc[:],
+                    lhsT=x_codes[:, i, cols].bitcast(FP8X4),
+                    lhsT_scale=x_scales[:, i, cols],
+                    rhs=wd_codes[:, g, :].bitcast(FP8X4),
+                    rhs_scale=wd_scales[:, g, :],
+                    start=(g == 0),
+                    stop=(g == DOWN_PASSES - 1),
                 )
-                stds[i] = std
-            centreds = {}
-            for i in tiles:
-                centred = ln.tile([P, LATENT], F32, tag="centred")
-                nc.vector.scalar_tensor_tensor(
-                    out=centred[:], in0=accs[i][:], scalar=means[i][:, 0:1], in1=gain,
-                    op0=ALU.subtract, op1=ALU.mult,
-                )
-                centreds[i] = centred
-            rstds = {}
-            for i in tiles:
-                rstd = small.tile([P, 1], F32, tag="rstd")
-                nc.vector.reciprocal(out=rstd[:], in_=stds[i][:])
-                rstds[i] = rstd
-            latents = {}
-            for i in tiles:
-                latent = ln.tile([P, LATENT], BF16, tag="latent")
-                nc.vector.scalar_tensor_tensor(
-                    out=latent[:], in0=centreds[i][:], scalar=rstds[i][:], in1=bias,
-                    op0=ALU.mult, op1=ALU.add,
-                )
-                latents[i] = latent
-            groupeds = {}
-            for i in tiles:
-                flipped = psum_t.tile([P, PACK, P], BF16, tag="flip")
-                for j in range(PACK):
-                    nc.tensor.transpose(
-                        flipped[:, j, :], latents[i][:, j * P : (j + 1) * P], ident_bf16[:]
-                    )
-                c_grouped = stage.tile([P, P, PACK], BF16, tag="c_grouped", bufs=4, align_bytes=64)
-                nc.scalar.copy(out=c_grouped[:], in_=flipped[:].rearrange("p j r -> p r j"))
-                groupeds[i] = c_grouped
-            for i in tiles:
-                quantise(nc, groupeds[i], c_codes[:, i, :], c_scales[:, i, :])
+            stats = small.tile([P, 6], F32, tag="stats")
+            nc.vector.bn_stats(out=stats[:], in_=acc[:])
+            mean_var = small.tile([P, 2], F32, tag="mean_var")
+            nc.vector.bn_aggr(out=mean_var[:], in_=stats[:])
+            centred = ln.tile([P, LATENT], F32, tag="centred")
+            nc.vector.scalar_tensor_tensor(
+                out=centred[:], in0=acc[:], scalar=mean_var[:, 0:1], in1=gain,
+                op0=ALU.subtract, op1=ALU.mult,
+            )
+            std = small.tile([P, 1], F32, tag="std")
+            nc.scalar.activation(out=std[:], in_=mean_var[:, 1:2], func=ACT.Sqrt, bias=eps[:], scale=1.0)
+            rstd = small.tile([P, 1], F32, tag="rstd")
+            nc.vector.reciprocal(out=rstd[:], in_=std[:])
+            latent = ln.tile([P, LATENT], BF16, tag="latent")
+            nc.vector.scalar_tensor_tensor(
+                out=latent[:], in0=centred[:], scalar=rstd[:], in1=bias,
+                op0=ALU.mult, op1=ALU.add,
+            )
+            flipped = psum_t.tile([P, PACK, P], BF16, tag="flip")
+            for j in range(PACK):
+                nc.tensor.transpose(flipped[:, j, :], latent[:, j * P : (j + 1) * P], ident_bf16[:])
+            c_grouped = stage.tile([P, P, PACK], BF16, tag="c_grouped", bufs=2, align_bytes=64)
+            nc.scalar.copy(out=c_grouped[:], in_=flipped[:].rearrange("p j r -> p r j"))
+            nc.vector.quantize_mx(
+                out=c_codes[:, i, :].bitcast(FP8X4),
+                scales=c_scales[:, i, :],
+                in_=c_grouped[:].rearrange("p r j -> p (r j)"),
+            )
 
         def project_up(i, first_chunk, chunks, vector_share, c_codes, c_scales, wu_codes, wu_scales, out_view):
             staging = outp.tile([P, chunks * N_TILE], F32, tag="staging")
@@ -270,45 +235,35 @@ def tile_transformerdecoderblock_pa_kernel(
                 out=out_view[:, i, first_col : first_col + chunks * N_TILE], in_=staging[:]
             )
 
+        quantise_down_piece(0, False, wdq_raw, wdq_codes, wdq_scales)
+        quantise_down_piece(1, False, wdq_raw, wdq_codes, wdq_scales)
         quantise_token_tile(0)
-        quantise_pieces(
-            nc, stage, [down_piece(g, False, wdq_raw, wdq_codes, wdq_scales) for g in range(DOWN_PASSES)]
-        )
-        for i in range(1, TOKEN_TILES):
-            quantise_token_tile(i)
-        for tiles in ((0, 1), (2, 3)):
-            latent_tiles(
-                tiles, wdq_codes, wdq_scales, spread[:, 0, :], spread[:, 1, :], cq_codes, cq_scales
-            )
-        quantise_pieces(
-            nc, stage,
-            [up_piece(c, c == 1, wuq_raw, wuq_codes, wuq_scales) for c in range(D_MODEL // N_TILE)],
-        )
-        quantise_pieces(
-            nc, stage, [down_piece(g, True, wdkv_raw, wdkv_codes, wdkv_scales) for g in range(DOWN_PASSES)]
-        )
-        for tiles in ((0, 1), (2, 3)):
-            latent_tiles(
-                tiles, wdkv_codes, wdkv_scales, spread[:, 2, :], spread[:, 3, :], ckv_codes, ckv_scales
-            )
+        quantise_down_piece(2, False, wdq_raw, wdq_codes, wdq_scales)
+        quantise_down_piece(3, False, wdq_raw, wdq_codes, wdq_scales)
+        quantise_token_tile(1)
+        for i in range(TOKEN_TILES):
+            if i + 2 < TOKEN_TILES:
+                quantise_token_tile(i + 2)
+            latent_tile(i, wdq_codes, wdq_scales, spread[:, 0, :], spread[:, 1, :], cq_codes, cq_scales)
+        for g in range(DOWN_PASSES):
+            quantise_down_piece(g, True, wdkv_raw, wdkv_codes, wdkv_scales)
+        for c in range(D_MODEL // N_TILE):
+            quantise_up_piece(c, c % 2 == 1, wuq_raw, wuq_codes, wuq_scales)
+        for i in range(TOKEN_TILES):
+            latent_tile(i, wdkv_codes, wdkv_scales, spread[:, 2, :], spread[:, 3, :], ckv_codes, ckv_scales)
         for i in range(TOKEN_TILES):
             for first_chunk in range(0, D_MODEL // N_TILE, STORE_CHUNKS):
                 project_up(
                     i, first_chunk, STORE_CHUNKS, False,
                     cq_codes, cq_scales, wuq_codes, wuq_scales, q_view,
                 )
-        kv_chunks = 2 * D_MODEL // N_TILE
-        kv_pieces = [up_piece(c, False, wukv_raw, wukv_codes, wukv_scales) for c in range(kv_chunks)]
-        kv_grouped = {}
-        for c in range(STORE_CHUNKS):
-            kv_grouped[c] = regroup(nc, stage, False, kv_pieces[c][1])
-        for first_chunk in range(0, kv_chunks, STORE_CHUNKS):
+        kv_groups = 2 * D_MODEL // (STORE_CHUNKS * N_TILE)
+        for group in range(kv_groups):
+            first_chunk = group * STORE_CHUNKS
             for c in range(first_chunk, first_chunk + STORE_CHUNKS):
-                quantise(nc, kv_grouped[c], kv_pieces[c][2], kv_pieces[c][3])
-                if c + STORE_CHUNKS < kv_chunks:
-                    kv_grouped[c + STORE_CHUNKS] = regroup(nc, stage, False, kv_pieces[c + STORE_CHUNKS][1])
+                quantise_up_piece(c, False, wukv_raw, wukv_codes, wukv_scales)
             for i in range(TOKEN_TILES):
                 project_up(
-                    i, first_chunk, STORE_CHUNKS, first_chunk + STORE_CHUNKS == kv_chunks,
+                    i, first_chunk, STORE_CHUNKS, group == kv_groups - 1,
                     ckv_codes, ckv_scales, wukv_codes, wukv_scales, kv_view,
                 )

@@ -75,19 +75,17 @@ def tile_transformerdecoderblock_pa_kernel(
         nc.vector.memset(vector_row[:], 0.0)
         ident_f32 = const.tile([P, P], F32)
         make_identity(nc, ident_f32[:])
-        ident_bf16 = const.tile([P, P], BF16)
-        make_identity(nc, ident_bf16[:])
 
         x_raw = raw.tile([P, TOKEN_TILES, D_MODEL], BF16)
         wdq_raw = raw.tile([P, 2 * DOWN_PASSES, 2 * LATENT], BF16)
         wdkv_raw = raw.tile([P, 2 * DOWN_PASSES, 2 * LATENT], BF16)
-        wuq_raw = raw.tile([P, PACK, D_MODEL], BF16)
-        wukv_raw = raw.tile([P, PACK, 2 * D_MODEL], BF16)
+        wuq_raw = raw.tile([P, 2, 2 * D_MODEL], BF16)
+        wukv_raw = raw.tile([P, 2, 4 * D_MODEL], BF16)
 
         wdq_view = W_dq.rearrange("(a p e) n -> p a (e n)", a=2 * DOWN_PASSES, p=P, e=2)
         wdkv_view = W_dkv.rearrange("(a p e) n -> p a (e n)", a=2 * DOWN_PASSES, p=P, e=2)
-        wuq_view = W_uq.rearrange("(j p) n -> p j n", j=PACK, p=P)
-        wukv_view = W_ukv.rearrange("(j p) n -> p j n", j=PACK, p=P)
+        wuq_view = W_uq.rearrange("(u p e) n -> p u (e n)", u=2, p=P, e=2)
+        wukv_view = W_ukv.rearrange("(u p e) n -> p u (e n)", u=2, p=P, e=2)
 
         nc.sync.dma_start(out=wdq_raw[:, 0:2, :], in_=wdq_view[:, 0:2, :])
         nc.sync.dma_start(out=x_raw[:, 0:1, :], in_=x_view[:, 0:1, :])
@@ -106,11 +104,12 @@ def tile_transformerdecoderblock_pa_kernel(
         for half in range(2):
             rows = slice(4 * half, 4 * half + 4)
             nc.sync.dma_start(out=wdkv_raw[:, rows, :], in_=wdkv_view[:, rows, :])
-        for half in range(2):
-            rows = slice(2 * half, 2 * half + 2)
-            nc.sync.dma_start(out=wuq_raw[:, rows, :], in_=wuq_view[:, rows, :])
-        for j in range(PACK):
-            nc.sync.dma_start(out=wukv_raw[:, j : j + 1, :], in_=wukv_view[:, j : j + 1, :])
+        for u in range(2):
+            nc.sync.dma_start(out=wuq_raw[:, u : u + 1, :], in_=wuq_view[:, u : u + 1, :])
+        for u in range(2):
+            for e in range(2):
+                cols = slice(2 * D_MODEL * e, 2 * D_MODEL * (e + 1))
+                nc.sync.dma_start(out=wukv_raw[:, u : u + 1, cols], in_=wukv_view[:, u : u + 1, cols])
 
         x_codes = keep.tile([P, TOKEN_TILES, DOWN_PASSES * P], U32, align_bytes=64)
         x_scales = keep.tile([P, TOKEN_TILES, DOWN_PASSES * P], U8, align_bytes=64)
@@ -166,7 +165,7 @@ def tile_transformerdecoderblock_pa_kernel(
             quantise_weight_piece(nc, stage, on_scalar, rows, wd_codes[:, g, :], wd_scales[:, g, :])
 
         def quantise_up_piece(c, on_scalar, wu_raw, wu_codes, wu_scales):
-            rows = wu_raw[:, :, c * N_TILE : (c + 1) * N_TILE]
+            rows = wu_raw.rearrange("p u (e n) -> p (u e) n", e=2)[:, :, c * N_TILE : (c + 1) * N_TILE]
             quantise_weight_piece(nc, stage, on_scalar, rows, wu_codes[:, c, :], wu_scales[:, c, :])
 
         def latent_tile(i, wd_codes, wd_scales, gain, bias, c_codes, c_scales):
@@ -200,15 +199,19 @@ def tile_transformerdecoderblock_pa_kernel(
                 out=latent[:], in0=centred[:], scalar=rstd[:], in1=bias,
                 op0=ALU.mult, op1=ALU.add,
             )
-            flipped = psum_t.tile([P, PACK, P], BF16, tag="flip")
-            for j in range(PACK):
-                nc.tensor.transpose(flipped[:, j, :], latent[:, j * P : (j + 1) * P], ident_bf16[:])
-            c_grouped = stage.tile([P, P, PACK], BF16, tag="c_grouped", bufs=2, align_bytes=64)
-            nc.scalar.copy(out=c_grouped[:], in_=flipped[:].rearrange("p j r -> p r j"))
+            words = latent[:].bitcast(F32)
+            flipped = psum_t.tile([P, 2, P], F32, tag="flip")
+            for u in range(2):
+                nc.tensor.transpose(flipped[:, u, :], words[:, u * P : (u + 1) * P], ident_f32[:])
+            c_grouped = stage.tile([P, P * PACK], BF16, tag="c_grouped", bufs=2, align_bytes=64)
+            nc.scalar.copy(
+                out=c_grouped[:].bitcast(F32).rearrange("p (r u) -> p r u", u=2),
+                in_=flipped[:].rearrange("p u r -> p r u"),
+            )
             nc.vector.quantize_mx(
                 out=c_codes[:, i, :].bitcast(FP8X4),
                 scales=c_scales[:, i, :],
-                in_=c_grouped[:].rearrange("p r j -> p (r j)"),
+                in_=c_grouped[:],
             )
 
         def project_up(i, first_chunk, chunks, vector_share, c_codes, c_scales, wu_codes, wu_scales, out_view):
@@ -248,7 +251,7 @@ def tile_transformerdecoderblock_pa_kernel(
         for g in range(DOWN_PASSES):
             quantise_down_piece(g, True, wdkv_raw, wdkv_codes, wdkv_scales)
         for c in range(D_MODEL // N_TILE):
-            quantise_up_piece(c, c % 2 == 1, wuq_raw, wuq_codes, wuq_scales)
+            quantise_up_piece(c, c % 2 == 1, wuq_raw[:], wuq_codes, wuq_scales)
         for i in range(TOKEN_TILES):
             latent_tile(i, wdkv_codes, wdkv_scales, spread[:, 2, :], spread[:, 3, :], ckv_codes, ckv_scales)
         for i in range(TOKEN_TILES):
@@ -261,7 +264,7 @@ def tile_transformerdecoderblock_pa_kernel(
         for group in range(kv_groups):
             first_chunk = group * STORE_CHUNKS
             for c in range(first_chunk, first_chunk + STORE_CHUNKS):
-                quantise_up_piece(c, False, wukv_raw, wukv_codes, wukv_scales)
+                quantise_up_piece(c, False, wukv_raw[:], wukv_codes, wukv_scales)
             for i in range(TOKEN_TILES):
                 project_up(
                     i, first_chunk, STORE_CHUNKS, group == kv_groups - 1,

@@ -68,7 +68,7 @@ def tile_transformerdecoderblock_pa_kernel(
         eps = const.tile([P, 1], F32)
         nc.vector.memset(eps[:], EPS)
         warm = const.tile([P, 1], F32)
-        nc.scalar.activation(out=warm[:], in_=eps[:], func=ACT.Sqrt)
+        nc.scalar.activation(out=warm[:], in_=eps[:], func=ACT.Abs_reciprocal_sqrt)
         ones = const.tile([P, P], BF16)
         nc.vector.memset(ones[:], 1.0)
         vector_row = const.tile([P, 4 * LATENT], BF16)
@@ -190,10 +190,10 @@ def tile_transformerdecoderblock_pa_kernel(
                 out=centred[:], in0=acc[:], scalar=mean_var[:, 0:1], in1=gain,
                 op0=ALU.subtract, op1=ALU.mult,
             )
-            std = small.tile([P, 1], F32, tag="std")
-            nc.scalar.activation(out=std[:], in_=mean_var[:, 1:2], func=ACT.Sqrt, bias=eps[:], scale=1.0)
             rstd = small.tile([P, 1], F32, tag="rstd")
-            nc.vector.reciprocal(out=rstd[:], in_=std[:])
+            nc.scalar.activation(
+                out=rstd[:], in_=mean_var[:, 1:2], func=ACT.Abs_reciprocal_sqrt, bias=eps[:], scale=1.0
+            )
             latent = ln.tile([P, LATENT], BF16, tag="latent")
             nc.vector.scalar_tensor_tensor(
                 out=latent[:], in0=centred[:], scalar=rstd[:], in1=bias,

@@ -126,18 +126,6 @@ def tile_transformerdecoderblock_pa_kernel(
         ckv_codes = keep.tile([P, TOKEN_TILES, P], U32, align_bytes=64)
         ckv_scales = keep.tile([P, TOKEN_TILES, P], U8, align_bytes=64)
 
-        spread = const.tile([P, 4, LATENT], BF16)
-        for v in range(4):
-            spread_ps = psum_t.tile([P, LATENT], F32, tag="flip")
-            nc.tensor.matmul(
-                out=spread_ps[:],
-                lhsT=ones[:],
-                rhs=vector_row[:, v * LATENT : (v + 1) * LATENT],
-                start=True,
-                stop=True,
-            )
-            nc.scalar.copy(out=spread[:, v, :], in_=spread_ps[:])
-
         def quantise_token_tile(i):
             words = x_raw[:, i, :].bitcast(F32)
             x_grouped = stage.tile([P, DOWN_PASSES * P * PACK], BF16, tag="grouped", align_bytes=64)
@@ -241,6 +229,17 @@ def tile_transformerdecoderblock_pa_kernel(
         quantise_down_piece(0, False, wdq_raw, wdq_codes, wdq_scales)
         quantise_down_piece(1, False, wdq_raw, wdq_codes, wdq_scales)
         quantise_token_tile(0)
+        spread = const.tile([P, 4, LATENT], BF16)
+        for v in range(4):
+            spread_ps = psum_t.tile([P, LATENT], F32, tag="flip")
+            nc.tensor.matmul(
+                out=spread_ps[:],
+                lhsT=ones[:],
+                rhs=vector_row[:, v * LATENT : (v + 1) * LATENT],
+                start=True,
+                stop=True,
+            )
+            nc.scalar.copy(out=spread[:, v, :], in_=spread_ps[:])
         quantise_down_piece(2, False, wdq_raw, wdq_codes, wdq_scales)
         quantise_down_piece(3, False, wdq_raw, wdq_codes, wdq_scales)
         quantise_token_tile(1)

from contextlib import ExitStack

import concourse.mybir as mybir
from concourse.masks import make_identity

F32 = mybir.dt.float32
BF16 = mybir.dt.bfloat16
U32 = mybir.dt.uint32
U8 = mybir.dt.uint8
FP8X4 = mybir.dt.float8_e4m3fn_x4
ALU = mybir.AluOpType
ACT = mybir.ActivationFunctionType

P = 128
PACK = 4
K_PASS = P * PACK
TOKENS = 512
D_MODEL = 2048
LATENT = 512
TOKEN_TILES = TOKENS // P
DOWN_PASSES = D_MODEL // K_PASS
N_TILE = 512
STORE_CHUNKS = 2
EPS = 1e-5

FLOPS = 2 * TOKENS * D_MODEL * LATENT * 2 + 2 * TOKENS * LATENT * (D_MODEL + 2 * D_MODEL)


def regroup(nc, on_scalar, grouped, rows):
    dst = grouped.rearrange("p (c i) t -> p c t i", i=4)
    src = rows.rearrange("p t (c i) -> p c t i", i=4)
    if on_scalar:
        nc.scalar.copy(out=dst, in_=src)
    else:
        nc.vector.tensor_copy(out=dst, in_=src)


def quantise_weight_piece(nc, stage, on_scalar, rows, codes, scales):
    grouped = stage.tile([P, N_TILE, PACK], BF16, tag="grouped", align_bytes=64)
    regroup(nc, on_scalar, grouped[:], rows)
    nc.vector.quantize_mx(
        out=codes.bitcast(FP8X4),
        scales=scales,
        in_=grouped[:].rearrange("p n t -> p (n t)"),
    )


def tile_transformerdecoderblock_pa_kernel(
    tc, normed, W_dq, q_ln_g, q_ln_b, W_uq, W_dkv, kv_ln_g, kv_ln_b, W_ukv, out_0, out_1
):
    nc = tc.nc
    with ExitStack() as ctx:
        const = ctx.enter_context(tc.tile_pool(name="const", bufs=1))
        raw = ctx.enter_context(tc.tile_pool(name="raw", bufs=1))
        keep = ctx.enter_context(tc.tile_pool(name="keep", bufs=1))
        stage = ctx.enter_context(tc.tile_pool(name="stage", bufs=6))
        ln = ctx.enter_context(tc.tile_pool(name="ln", bufs=2))
        small = ctx.enter_context(tc.tile_pool(name="small", bufs=4))
        outp = ctx.enter_context(tc.tile_pool(name="outp", bufs=6))
        psum_t = ctx.enter_context(tc.psum_pool(name="psum_t", bufs=3))
        psum_acc = ctx.enter_context(tc.psum_pool(name="psum_acc", bufs=2))
        psum_out = ctx.enter_context(tc.psum_pool(name="psum_out", bufs=3))

        x_view = normed.flatten_outer_dims().rearrange("(p i) d -> p i d", i=TOKEN_TILES)
        q_view = out_0.flatten_outer_dims().rearrange("(p i) n -> p i n", i=TOKEN_TILES)
        kv_view = out_1.flatten_outer_dims().rearrange("(p i) n -> p i n", i=TOKEN_TILES)

        eps = const.tile([P, 1], F32)
        nc.vector.memset(eps[:], EPS)
        warm = const.tile([P, 1], F32)
        nc.scalar.activation(out=warm[:], in_=eps[:], func=ACT.Abs_reciprocal_sqrt)
        ones = const.tile([P, P], BF16)
        nc.vector.memset(ones[:], 1.0)
        vector_row = const.tile([P, 4 * LATENT], BF16)
        nc.vector.memset(vector_row[:], 0.0)
        ident_f32 = const.tile([P, P], F32)
        make_identity(nc, ident_f32[:])

        x_raw = raw.tile([P, TOKEN_TILES, D_MODEL], BF16)
        wdq_raw = raw.tile([P, 2 * DOWN_PASSES, 2 * LATENT], BF16)
        wdkv_raw = raw.tile([P, 2 * DOWN_PASSES, 2 * LATENT], BF16)
        wuq_raw = raw.tile([P, 2, 2 * D_MODEL], BF16)
        wukv_raw = raw.tile([P, 2, 4 * D_MODEL], BF16)

        wdq_view = W_dq.rearrange("(a p e) n -> p a (e n)", a=2 * DOWN_PASSES, p=P, e=2)
        wdkv_view = W_dkv.rearrange("(a p e) n -> p a (e n)", a=2 * DOWN_PASSES, p=P, e=2)
        wuq_view = W_uq.rearrange("(u p e) n -> p u (e n)", u=2, p=P, e=2)
        wukv_view = W_ukv.rearrange("(u p e) n -> p u (e n)", u=2, p=P, e=2)

        nc.sync.dma_start(out=wdq_raw[:, 0:2, :], in_=wdq_view[:, 0:2, :])
        nc.sync.dma_start(out=x_raw[:, 0:1, :], in_=x_view[:, 0:1, :])
        vector_in = const.tile([1, 4 * LATENT], BF16)
        for v, vec in enumerate((q_ln_g, q_ln_b, kv_ln_g, kv_ln_b)):
            nc.sync.dma_start(
                out=vector_in[0:1, v * LATENT : (v + 1) * LATENT],
                in_=vec.rearrange("(o n) -> o n", o=1),
            )
        nc.vector.tensor_copy(out=vector_row[0:1, :], in_=vector_in[:])
        nc.sync.dma_start(out=wdq_raw[:, 2:4, :], in_=wdq_view[:, 2:4, :])
        nc.sync.dma_start(out=wdq_raw[:, 4:6, :], in_=wdq_view[:, 4:6, :])
        nc.sync.dma_start(out=wdq_raw[:, 6:8, :], in_=wdq_view[:, 6:8, :])
        nc.sync.dma_start(out=x_raw[:, 1:2, :], in_=x_view[:, 1:2, :])
        nc.sync.dma_start(out=x_raw[:, 2:4, :], in_=x_view[:, 2:4, :])
        for half in range(2):
            rows = slice(4 * half, 4 * half + 4)
            nc.sync.dma_start(out=wdkv_raw[:, rows, :], in_=wdkv_view[:, rows, :])
        for u in range(2):
            nc.sync.dma_start(out=wuq_raw[:, u : u + 1, :], in_=wuq_view[:, u : u + 1, :])
        for u in range(2):
            for e in range(2):
                cols = slice(2 * D_MODEL * e, 2 * D_MODEL * (e + 1))
                nc.sync.dma_start(out=wukv_raw[:, u : u + 1, cols], in_=wukv_view[:, u : u + 1, cols])

        x_codes = keep.tile([P, TOKEN_TILES, DOWN_PASSES * P], U32, align_bytes=64)
        x_scales = keep.tile([P, TOKEN_TILES, DOWN_PASSES * P], U8, align_bytes=64)
        wdq_codes = keep.tile([P, DOWN_PASSES, LATENT], U32, align_bytes=64)
        wdq_scales = keep.tile([P, DOWN_PASSES, LATENT], U8, align_bytes=64)
        wdkv_codes = keep.tile([P, DOWN_PASSES, LATENT], U32, align_bytes=64)
        wdkv_scales = keep.tile([P, DOWN_PASSES, LATENT], U8, align_bytes=64)
        wuq_codes = keep.tile([P, D_MODEL // N_TILE, N_TILE], U32, align_bytes=64)
        wuq_scales = keep.tile([P, D_MODEL // N_TILE, N_TILE], U8, align_bytes=64)
        wukv_codes = keep.tile([P, 2 * D_MODEL // N_TILE, N_TILE], U32, align_bytes=64)
        wukv_scales = keep.tile([P, 2 * D_MODEL // N_TILE, N_TILE], U8, align_bytes=64)
        cq_codes = keep.tile([P, TOKEN_TILES, P], U32, align_bytes=64)
        cq_scales = keep.tile([P, TOKEN_TILES, P], U8, align_bytes=64)
        ckv_codes = keep.tile([P, TOKEN_TILES, P], U32, align_bytes=64)
        ckv_scales = keep.tile([P, TOKEN_TILES, P], U8, align_bytes=64)

        def quantise_token_tile(i):
            words = x_raw[:, i, :].bitcast(F32)
            x_grouped = stage.tile([P, DOWN_PASSES * P * PACK], BF16, tag="grouped", align_bytes=64)
            grouped_words = x_grouped[:].bitcast(F32).rearrange(
                "p (g r u) -> p g r u", g=DOWN_PASSES, r=P, u=2
            )
            for half in range(2):
                flipped = psum_t.tile([P, 2, 2, P], F32, tag="flip")
                for g_local in range(2):
                    for u in range(2):
                        first = (2 * (2 * half + g_local) + u) * P
                        nc.tensor.transpose(
                            flipped[:, g_local, u, :], words[:, first : first + P], ident_f32[:]
                        )
                nc.scalar.copy(
                    out=grouped_words[:, 2 * half : 2 * half + 2, :, :],
                    in_=flipped[:].rearrange("p g u r -> p g r u"),
                )
            nc.vector.quantize_mx(
                out=x_codes[:, i, :].bitcast(FP8X4), scales=x_scales[:, i, :], in_=x_grouped[:]
            )

        def quantise_down_piece(g, on_scalar, wd_raw, wd_codes, wd_scales):
            rows = wd_raw[:, 2 * g : 2 * g + 2, :].rearrange("p u (e n) -> p (u e) n", e=2)
            quantise_weight_piece(nc, stage, on_scalar, rows, wd_codes[:, g, :], wd_scales[:, g, :])

        def quantise_up_piece(c, on_scalar, wu_raw, wu_codes, wu_scales):
            rows = wu_raw.rearrange("p u (e n) -> p (u e) n", e=2)[:, :, c * N_TILE : (c + 1) * N_TILE]
            quantise_weight_piece(nc, stage, on_scalar, rows, wu_codes[:, c, :], wu_scales[:, c, :])

        def latent_tile(i, wd_codes, wd_scales, gain, bias, c_codes, c_scales):
            acc = psum_acc.tile([P, LATENT], F32, tag="acc")
            for g in range(DOWN_PASSES):
                cols = slice(g * P, (g + 1) * P)
                nc.tensor.matmul_mx(
                    out=acc[:],
                    lhsT=x_codes[:, i, cols].bitcast(FP8X4),
                    lhsT_scale=x_scales[:, i, cols],
                    rhs=wd_codes[:, g, :].bitcast(FP8X4),
                    rhs_scale=wd_scales[:, g, :],
                    start=(g == 0),
                    stop=(g == DOWN_PASSES - 1),
                )
            stats = small.tile([P, 6], F32, tag="stats")
            nc.vector.bn_stats(out=stats[:], in_=acc[:])
            mean_var = small.tile([P, 2], F32, tag="mean_var")
            nc.vector.bn_aggr(out=mean_var[:], in_=stats[:])
            centred = ln.tile([P, LATENT], F32, tag="centred")
            nc.vector.scalar_tensor_tensor(
                out=centred[:], in0=acc[:], scalar=mean_var[:, 0:1], in1=gain,
                op0=ALU.subtract, op1=ALU.mult,
            )
            rstd = small.tile([P, 1], F32, tag="rstd")
            nc.scalar.activation(
                out=rstd[:], in_=mean_var[:, 1:2], func=ACT.Abs_reciprocal_sqrt, bias=eps[:], scale=1.0
            )
            latent = ln.tile([P, LATENT], BF16, tag="latent")
            nc.vector.scalar_tensor_tensor(
                out=latent[:], in0=centred[:], scalar=rstd[:], in1=bias,
                op0=ALU.mult, op1=ALU.add,
            )
            words = latent[:].bitcast(F32)
            flipped = psum_t.tile([P, 2, P], F32, tag="flip")
            for u in range(2):
                nc.tensor.transpose(flipped[:, u, :], words[:, u * P : (u + 1) * P], ident_f32[:])
            c_grouped = stage.tile([P, P * PACK], BF16, tag="c_grouped", bufs=2, align_bytes=64)
            nc.scalar.copy(
                out=c_grouped[:].bitcast(F32).rearrange("p (r u) -> p r u", u=2),
                in_=flipped[:].rearrange("p u r -> p r u"),
            )
            nc.vector.quantize_mx(
                out=c_codes[:, i, :].bitcast(FP8X4),
                scales=c_scales[:, i, :],
                in_=c_grouped[:],
            )

        def project_up(i, first_chunk, chunks, vector_share, c_codes, c_scales, wu_codes, wu_scales, out_view):
            staging = outp.tile([P, chunks * N_TILE], F32, tag="staging")
            for h in range(chunks):
                chunk = first_chunk + h
                bank = psum_out.tile([P, N_TILE], F32, tag="bank")
                nc.tensor.matmul_mx(
                    out=bank[:],
                    lhsT=c_codes[:, i, :].bitcast(FP8X4),
                    lhsT_scale=c_scales[:, i, :],
                    rhs=wu_codes[:, chunk, :].bitcast(FP8X4),
                    rhs_scale=wu_scales[:, chunk, :],
                    start=True,
                    stop=True,
                )
                dst = staging[:, h * N_TILE : (h + 1) * N_TILE]
                if vector_share and h % 2 == 1:
                    nc.vector.tensor_copy(out=dst, in_=bank[:])
                else:
                    nc.scalar.copy(out=dst, in_=bank[:])
            first_col = first_chunk * N_TILE
            nc.sync.dma_start(
                out=out_view[:, i, first_col : first_col + chunks * N_TILE], in_=staging[:]
            )

        quantise_down_piece(0, False, wdq_raw, wdq_codes, wdq_scales)
        quantise_down_piece(1, False, wdq_raw, wdq_codes, wdq_scales)
        quantise_token_tile(0)
        spread = const.tile([P, 4, LATENT], BF16)
        for v in range(4):
            spread_ps = psum_t.tile([P, LATENT], F32, tag="flip")
            nc.tensor.matmul(
                out=spread_ps[:],
                lhsT=ones[:],
                rhs=vector_row[:, v * LATENT : (v + 1) * LATENT],
                start=True,
                stop=True,
            )
            nc.scalar.copy(out=spread[:, v, :], in_=spread_ps[:])
        quantise_down_piece(2, False, wdq_raw, wdq_codes, wdq_scales)
        quantise_down_piece(3, False, wdq_raw, wdq_codes, wdq_scales)
        quantise_token_tile(1)
        for i in range(TOKEN_TILES):
            if i + 2 < TOKEN_TILES:
                quantise_token_tile(i + 2)
            latent_tile(i, wdq_codes, wdq_scales, spread[:, 0, :], spread[:, 1, :], cq_codes, cq_scales)
        for g in range(DOWN_PASSES):
            quantise_down_piece(g, True, wdkv_raw, wdkv_codes, wdkv_scales)
        for c in range(D_MODEL // N_TILE):
            quantise_up_piece(c, c % 2 == 1, wuq_raw[:], wuq_codes, wuq_scales)
        for i in range(TOKEN_TILES):
            latent_tile(i, wdkv_codes, wdkv_scales, spread[:, 2, :], spread[:, 3, :], ckv_codes, ckv_scales)
        for i in range(TOKEN_TILES):
            for first_chunk in range(0, D_MODEL // N_TILE, STORE_CHUNKS):
                project_up(
                    i, first_chunk, STORE_CHUNKS, False,
                    cq_codes, cq_scales, wuq_codes, wuq_scales, q_view,
                )
        kv_groups = 2 * D_MODEL // (STORE_CHUNKS * N_TILE)
        for group in range(kv_groups):
            first_chunk = group * STORE_CHUNKS
            for c in range(first_chunk, first_chunk + STORE_CHUNKS):
                quantise_up_piece(c, False, wukv_raw[:], wukv_codes, wukv_scales)
            for i in range(TOKEN_TILES):
                project_up(
                    i, first_chunk, STORE_CHUNKS, group == kv_groups - 1,
                    ckv_codes, ckv_scales, wukv_codes, wukv_scales, kv_view,
                )
